import numpy as np
import ml_dtypes


def mxq(x, axis, fmt="e4m3"):
    dtype, down = {"e4m3": (ml_dtypes.float8_e4m3fn, 7), "e5m2": (ml_dtypes.float8_e5m2, 14)}[fmt]
    v = np.moveaxis(np.asarray(x, np.float32).astype(ml_dtypes.bfloat16).astype(np.float64), axis, -1)
    blocks = v.reshape(v.shape[:-1] + (-1, 32))
    amax = np.abs(blocks).max(-1, keepdims=True)
    byte = np.maximum(np.where(amax > 0, np.frexp(amax)[1] - 1 + 127, 0) - down, 1)
    scale = np.exp2(byte - 127.0)
    codes = (blocks / scale).astype(np.float32).astype(dtype).astype(np.float64)
    return np.moveaxis((codes * scale).reshape(v.shape), -1, axis)


WIDE = False


def mx_kscale(k):
    if not WIDE:
        return np.ones(k)
    levels = np.array([10, -10, 5, -5, 0])
    if k % 512:
        return np.exp2(np.random.permutation(np.resize(levels, k // 32))).repeat(32)
    a = np.empty((k // 512, 16))
    for p in range(k // 512):
        a[p, :8] = np.random.permutation(np.resize(levels, 8))
        for g in range(8):
            far = levels[np.abs(levels - a[p, g]) >= 10]
            a[p, g + 8] = far[np.random.randint(len(far))]
    return np.exp2(a.ravel()).repeat(32)


BF16 = ml_dtypes.bfloat16


def bf(x):
    return np.asarray(x, np.float32).astype(BF16)


def f64(x):
    return np.asarray(x).astype(np.float64)


E2M1 = np.array([0.0, 0.5, 1.0, 1.5, 2.0, 3.0, 4.0, 6.0, -0.0, -0.5, -1.0, -1.5, -2.0, -3.0, -4.0, -6.0])


def pack_weight(w, fmt):
    k, n = w.shape
    w = f64(bf(w)).reshape(k // 32, 32, n)
    amax = np.abs(w).max(1)
    if fmt == "e4m3":
        byte = np.frexp(amax)[1] - 1 + 127 - 7
    else:
        mant, ex = np.frexp(amax / 6.0)
        byte = np.where(mant > 0.5, ex, ex - 1) + 127
    byte = np.clip(np.where(amax > 0, byte, 1), 1, 254)
    scaled = (w * np.exp2(127.0 - byte)[:, None, :]).reshape(k, n).astype(np.float32)
    by_word = np.ascontiguousarray(scaled.reshape(k // 512, 128, 4, n).transpose(0, 1, 3, 2))
    if fmt == "e4m3":
        words = by_word.astype(ml_dtypes.float8_e4m3fn).view(np.uint8)
    else:
        c = by_word.astype(ml_dtypes.float4_e2m1fn).view(np.uint8) & 0xF
        words = c[..., 0::2] | (c[..., 1::2] << 4)
    return np.ascontiguousarray(words), np.ascontiguousarray(byte.astype(np.uint8).reshape(k // 512, 16, n))


def unpack_weight(words, scales, fmt):
    g, p, n, _ = words.shape
    if fmt == "e4m3":
        vals = np.ascontiguousarray(words).view(ml_dtypes.float8_e4m3fn).astype(np.float64)
    else:
        nib = np.empty((g, p, n, 4), np.uint8)
        nib[..., 0::2] = words & 0xF
        nib[..., 1::2] = words >> 4
        vals = E2M1[nib]
    vals = vals * np.repeat(np.exp2(scales.astype(np.float64) - 127.0), 8, axis=1)[..., None]
    return vals.transpose(0, 1, 3, 2).reshape(g * 512, n)


B, N, C, D = 2, 512, 512, 512
ETA, TAU = 1.0, 1.5
FMT = "e4m3"


def setup_inputs():
    s, t = mx_kscale(C), mx_kscale(D)
    a = 2.0 * (C / D) ** 0.25 / np.sqrt(C)
    H_t = bf(np.random.standard_normal((B, N, C)) * s)
    A_stat = bf(np.random.random((N, N)))
    M_mask = bf(np.random.random((N, N)) - 0.25)
    Wq = np.random.standard_normal((D, C)) * a * t[:, None] / s
    Wk = np.random.standard_normal((D, C)) * a / t[:, None] / s
    Wq_words, Wq_scales = pack_weight(np.ascontiguousarray(Wq.T), FMT)
    Wk_words, Wk_scales = pack_weight(np.ascontiguousarray(Wk.T), FMT)
    return {"H_t": H_t,
            "A_stat": A_stat,
            "M_mask": M_mask,
            "Wq_words": Wq_words,
            "Wq_scales": Wq_scales,
            "Wk_words": Wk_words,
            "Wk_scales": Wk_scales}


def reference(H_t, A_stat, M_mask, Wq_words, Wq_scales, Wk_words, Wk_scales):
    c = H_t.shape[-1]
    hq = mxq(f64(H_t), 2, "e4m3")
    Q = hq @ unpack_weight(Wq_words, Wq_scales, FMT)
    K = hq @ unpack_weight(Wk_words, Wk_scales, FMT)
    logits = (mxq(Q, 2, "e4m3") @ mxq(K, 2, "e4m3").transpose(0, 2, 1)) / (np.sqrt(c) * TAU)
    logits = 0.5 * (logits + logits.transpose(0, 2, 1))
    n = logits.shape[-1]
    eye = np.eye(n, dtype=bool)
    logits = np.where(eye[None, :, :], -np.inf, logits)
    A_bias = np.where(eye, 0.0, f64(A_stat))
    logits = logits + ETA * A_bias[None, :, :]
    logits = np.where((f64(M_mask) <= 0)[None, :, :], -np.inf, logits)
    e = np.exp(logits - logits.max(-1, keepdims=True))
    return e / e.sum(-1, keepdims=True)

@@ -1,0 +1,248 @@
+import math
+from contextlib import ExitStack
+
+import concourse.mybir as mybir
+from concourse.masks import make_identity
+
+F32 = mybir.dt.float32
+BF16 = mybir.dt.bfloat16
+I32 = mybir.dt.int32
+U32 = mybir.dt.uint32
+U8 = mybir.dt.uint8
+FP8X4 = mybir.dt.float8_e4m3fn_x4
+ALU = mybir.AluOpType
+ACT = mybir.ActivationFunctionType
+AXIS = mybir.AxisListType
+
+P = 128
+PACK = 4
+B, N, C, D = 2, 512, 512, 512
+NODE_BLOCKS = N // P
+TAU = 1.5
+HALF_SCALE = 0.5 / (math.sqrt(C) * TAU)
+EXCLUDED = -1.0e30
+Q_SIDE, K_SIDE = 0, 1
+PAIRS = 4
+LAG = 1
+PAIRS_AHEAD = 2
+
+FLOPS = 2 * B * N * C * (2 * D) + 2 * B * N * N * D
+
+
+def tile_dynamicgraphattention_kernel(
+    tc, H_t, A_stat, M_mask, Wq_words, Wq_scales, Wk_words, Wk_scales, out
+):
+    nc = tc.nc
+    with ExitStack() as ctx:
+        keep = ctx.enter_context(tc.tile_pool(name="keep", bufs=1))
+        rows = ctx.enter_context(tc.tile_pool(name="rows", bufs=B * NODE_BLOCKS))
+        stats = ctx.enter_context(tc.tile_pool(name="stats", bufs=B * NODE_BLOCKS))
+        psum_flip = ctx.enter_context(tc.psum_pool(name="psum_flip", bufs=2))
+        psum_proj = ctx.enter_context(tc.psum_pool(name="psum_proj", bufs=4))
+        psum_score = ctx.enter_context(tc.psum_pool(name="psum_score", bufs=2))
+        ctx.enter_context(tc.manual_schedule())
+
+        identity = keep.tile([P, P], F32)
+        make_identity(nc, identity[:])
+        planes_in = keep.tile([P, 2, D], U8, align_bytes=64)
+        nc.vector.memset(planes_in[:].rearrange("p w n -> p (w n)").bitcast(I32), 0)
+        warm = keep.tile([P, 1], F32)
+        nc.vector.memset(warm[:], 0.0)
+        nc.scalar.activation(out=warm[:], in_=warm[:], func=ACT.Exp)
+
+        h_sb = keep.tile([P, B, NODE_BLOCKS, C], BF16)
+        words_in = keep.tile([P, 2, D], U32, align_bytes=64)
+        m_sb = keep.tile([P, NODE_BLOCKS, N], BF16)
+        a_sb = keep.tile([P, NODE_BLOCKS, N], BF16)
+
+        def load_h(b):
+            nc.sync.dma_start(out=h_sb[:, b], in_=H_t[b].rearrange("(j p) c -> p j c", p=P))
+
+        def load_scales(side, scales):
+            by_r = scales[0].rearrange("(Q r) n -> r Q n", r=4)
+            for r in range(4):
+                nc.sync.dma_start(
+                    out=planes_in[r:P:32, side, :].bitcast(I32), in_=by_r[r].bitcast(I32)
+                )
+
+        def load_words(side, words):
+            nc.sync.dma_start(
+                out=words_in[:, side, :].bitcast(I32),
+                in_=words[0].rearrange("p n t -> p (n t)").bitcast(I32),
+            )
+
+        load_h(0)
+        load_scales(Q_SIDE, Wq_scales)
+        load_h(1)
+        load_words(Q_SIDE, Wq_words)
+        load_words(K_SIDE, Wk_words)
+        load_scales(K_SIDE, Wk_scales)
+        nc.sync.dma_start(out=m_sb[:], in_=M_mask.rearrange("(j p) m -> p j m", p=P))
+        nc.sync.dma_start(out=a_sb[:], in_=A_stat.rearrange("(j p) m -> p j m", p=P))
+
+        w_words = keep.tile([P, 2, D], U32, align_bytes=64)
+        w_planes = keep.tile([P, 2, D], U8, align_bytes=64)
+
+        def permute_columns(side):
+            nc.vector.tensor_copy(
+                out=w_words[:, side, :].bitcast(I32).rearrange("p (t q r) -> p t q r", t=PACK, r=8),
+                in_=words_in[:, side, :].bitcast(I32).rearrange("p (q t r) -> p t q r", t=PACK, r=8),
+            )
+            nc.vector.tensor_copy(
+                out=w_planes[:, side, :].bitcast(I32).rearrange("p (t q r) -> p t q r", t=PACK, r=2),
+                in_=planes_in[:, side, :].bitcast(I32).rearrange("p (q t r) -> p t q r", t=PACK, r=2),
+            )
+
+        h_pairs = keep.tile([P, B, N, 2], F32, align_bytes=64)
+        h_codes = keep.tile([P, B, N], U32, align_bytes=64)
+        h_plane = keep.tile([P, B, N], U8, align_bytes=64)
+
+        def flip_h(b, half):
+            flipped = psum_flip.tile([P, 2, 2 * P], F32)
+            for jj in range(2):
+                words = h_sb[:, b, 2 * half + jj, :].bitcast(F32)
+                for u in range(2):
+                    nc.tensor.transpose(
+                        flipped[:, u, jj * P : (jj + 1) * P], words[:, u : C // 2 : 2], identity[:]
+                    )
+            nodes = slice(2 * P * half, 2 * P * (half + 1))
+            copy = nc.vector.tensor_copy if half == 0 else nc.scalar.copy
+            copy(out=h_pairs[:, b, nodes, :], in_=flipped[:].rearrange("p u n -> p n u"))
+
+        def quantise_h(b, half):
+            nodes = slice(2 * P * half, 2 * P * (half + 1))
+            nc.vector.quantize_mx(
+                out=h_codes[:, b, nodes].bitcast(FP8X4),
+                scales=h_plane[:, b, nodes],
+                in_=h_pairs[:, b, nodes, :].rearrange("p n u -> p (n u)").bitcast(BF16),
+            )
+
+        qk_grouped = keep.tile([P, B, 2, N, PACK], BF16, align_bytes=64)
+        qk_codes = keep.tile([P, B, 2, N], U32, align_bytes=64)
+        qk_planes = keep.tile([P, B, 2, N], U8, align_bytes=64)
+
+        def project(b, bank, copy):
+            side, j = divmod(bank, NODE_BLOCKS)
+            nodes = slice(j * P, (j + 1) * P)
+            acc = psum_proj.tile([P, PACK, P], F32)
+            for t in range(PACK):
+                features = slice(t * P, (t + 1) * P)
+                nc.tensor.matmul_mx(
+                    out=acc[:, t, :],
+                    lhsT=w_words[:, side, features].bitcast(FP8X4),
+                    lhsT_scale=w_planes[:, side, features],
+                    rhs=h_codes[:, b, nodes].bitcast(FP8X4),
+                    rhs_scale=h_plane[:, b, nodes],
+                    start=True,
+                    stop=True,
+                )
+            copy(out=qk_grouped[:, b, side, nodes, :], in_=acc[:].rearrange("p t n -> p n t"))
+
+        def project_pair_on_scalar(b, pair):
+            project(b, 2 * pair, nc.scalar.copy)
+            project(b, 2 * pair + 1, nc.scalar.copy)
+
+        def quantise_pair(b, pair):
+            side, half = divmod(pair, 2)
+            nodes = slice(2 * P * half, 2 * P * (half + 1))
+            nc.vector.quantize_mx(
+                out=qk_codes[:, b, side, nodes].bitcast(FP8X4),
+                scales=qk_planes[:, b, side, nodes],
+                in_=qk_grouped[:, b, side, nodes, :].rearrange("p n t -> p (n t)"),
+            )
+
+        bias = keep.tile([P, NODE_BLOCKS, N], BF16)
+
+        def penalise_excluded():
+            nc.vector.tensor_scalar(
+                out=bias[:], in0=m_sb[:], scalar1=0.0, scalar2=EXCLUDED, op0=ALU.is_le, op1=ALU.mult
+            )
+
+        def add_a_stat():
+            for j in range(NODE_BLOCKS):
+                diagonal = a_sb[:, j, j * P : (j + 1) * P]
+                nc.gpsimd.affine_select(
+                    out=diagonal,
+                    in_=diagonal,
+                    compare_op=ALU.not_equal,
+                    fill=EXCLUDED,
+                    base=0,
+                    pattern=[[-1, P]],
+                    channel_multiplier=1,
+                )
+            nc.vector.tensor_tensor(out=bias[:], in0=bias[:], in1=a_sb[:], op=ALU.add)
+
+        logits, neg_max, weights, row_sum = {}, {}, {}, {}
+
+        def logits_and_max(i, b, j):
+            nodes = slice(j * P, (j + 1) * P)
+            score = psum_score.tile([P, N], F32)
+            for first, (still, moving) in enumerate(((Q_SIDE, K_SIDE), (K_SIDE, Q_SIDE))):
+                nc.tensor.matmul_mx(
+                    out=score[:],
+                    lhsT=qk_codes[:, b, still, nodes].bitcast(FP8X4),
+                    lhsT_scale=qk_planes[:, b, still, nodes],
+                    rhs=qk_codes[:, b, moving, :].bitcast(FP8X4),
+                    rhs_scale=qk_planes[:, b, moving, :],
+                    start=(first == 0),
+                    stop=(first == 1),
+                )
+            logits[i] = rows.tile([P, N], F32, name="logits")
+            nc.vector.scalar_tensor_tensor(
+                out=logits[i][:], in0=score[:], scalar=HALF_SCALE, in1=bias[:, j, :], op0=ALU.mult, op1=ALU.add
+            )
+            neg_max[i] = stats.tile([P, 1], F32, name="neg_max")
+            nc.vector.tensor_reduce(out=neg_max[i][:], in_=logits[i][:], axis=AXIS.X, op=ALU.max, negate=True)
+
+        def exponentials(i):
+            weights[i] = rows.tile([P, N], F32, name="weights")
+            row_sum[i] = stats.tile([P, 1], F32, name="row_sum")
+            nc.scalar.activation(
+                out=weights[i][:],
+                in_=logits[i][:],
+                func=ACT.Exp,
+                bias=neg_max[i][:],
+                scale=1.0,
+                accum_out=row_sum[i][:],
+            )
+
+        def normalise_and_store(i):
+            b, j = divmod(i, NODE_BLOCKS)
+            inv_sum = stats.tile([P, 1], F32)
+            nc.vector.reciprocal(out=inv_sum[:], in_=row_sum[i][:])
+            nc.gpsimd.tensor_scalar(
+                out=weights[i][:], in0=weights[i][:], scalar1=inv_sum[:], scalar2=0.0, op0=ALU.mult, op1=ALU.add
+            )
+            nc.sync.dma_start(out=out[b, j * P : (j + 1) * P, :], in_=weights[i][:])
+
+        for b in range(B):
+            for half in range(2):
+                flip_h(b, half)
+            for half in range(2):
+                quantise_h(b, half)
+        for side in (Q_SIDE, K_SIDE):
+            permute_columns(side)
+        for pair in range(PAIRS):
+            if pair == PAIRS - 1:
+                penalise_excluded()
+            project(0, 2 * pair, nc.scalar.copy)
+            project(0, 2 * pair + 1, nc.scalar.copy if pair % 2 == 0 else nc.vector.tensor_copy)
+            if pair > 0:
+                quantise_pair(0, pair - 1)
+        quantise_pair(0, PAIRS - 1)
+        add_a_stat()
+        for pair in range(PAIRS_AHEAD):
+            project_pair_on_scalar(1, pair)
+        for i in range(B * NODE_BLOCKS):
+            b, j = divmod(i, NODE_BLOCKS)
+            logits_and_max(i, b, j)
+            if i >= LAG:
+                normalise_and_store(i - LAG)
+            if PAIRS_AHEAD + i < PAIRS:
+                project_pair_on_scalar(1, PAIRS_AHEAD + i)
+            exponentials(i)
+            if i in (1, 2):
+                quantise_pair(1, 2 * i - 2)
+                quantise_pair(1, 2 * i - 1)
+        for i in range(B * NODE_BLOCKS - LAG, B * NODE_BLOCKS):
+            normalise_and_store(i)

@@ -22,9 +22,7 @@ TAU = 1.5
 HALF_SCALE = 0.5 / (math.sqrt(C) * TAU)
 EXCLUDED = -1.0e30
 Q_SIDE, K_SIDE = 0, 1
-PAIRS = 4
-LAG = 1
-PAIRS_AHEAD = 2
+ROW_BLOCKS = B * NODE_BLOCKS
 
 FLOPS = 2 * B * N * C * (2 * D) + 2 * B * N * N * D
 
@@ -35,11 +33,8 @@ def tile_dynamicgraphattention_kernel(
     nc = tc.nc
     with ExitStack() as ctx:
         keep = ctx.enter_context(tc.tile_pool(name="keep", bufs=1))
-        rows = ctx.enter_context(tc.tile_pool(name="rows", bufs=B * NODE_BLOCKS))
-        stats = ctx.enter_context(tc.tile_pool(name="stats", bufs=B * NODE_BLOCKS))
-        psum_flip = ctx.enter_context(tc.psum_pool(name="psum_flip", bufs=2))
-        psum_proj = ctx.enter_context(tc.psum_pool(name="psum_proj", bufs=4))
-        psum_score = ctx.enter_context(tc.psum_pool(name="psum_score", bufs=2))
+        rows = ctx.enter_context(tc.tile_pool(name="rows", bufs=ROW_BLOCKS))
+        psum = ctx.enter_context(tc.psum_pool(name="psum", bufs=8))
         ctx.enter_context(tc.manual_schedule())
 
         identity = keep.tile([P, P], F32)
@@ -55,8 +50,10 @@ def tile_dynamicgraphattention_kernel(
         m_sb = keep.tile([P, NODE_BLOCKS, N], BF16)
         a_sb = keep.tile([P, NODE_BLOCKS, N], BF16)
 
-        def load_h(b):
-            nc.sync.dma_start(out=h_sb[:, b], in_=H_t[b].rearrange("(j p) c -> p j c", p=P))
+        def load_h(b, j0, j1):
+            nc.sync.dma_start(
+                out=h_sb[:, b, j0:j1], in_=H_t[b, j0 * P : j1 * P].rearrange("(j p) c -> p j c", p=P)
+            )
 
         def load_scales(side, scales):
             by_r = scales[0].rearrange("(Q r) n -> r Q n", r=4)
@@ -71,13 +68,14 @@ def tile_dynamicgraphattention_kernel(
                 in_=words[0].rearrange("p n t -> p (n t)").bitcast(I32),
             )
 
-        load_h(0)
+        load_h(0, 0, 2)
         load_scales(Q_SIDE, Wq_scales)
-        load_h(1)
         load_words(Q_SIDE, Wq_words)
-        load_words(K_SIDE, Wk_words)
-        load_scales(K_SIDE, Wk_scales)
+        load_h(0, 2, 4)
         nc.sync.dma_start(out=m_sb[:], in_=M_mask.rearrange("(j p) m -> p j m", p=P))
+        load_scales(K_SIDE, Wk_scales)
+        load_words(K_SIDE, Wk_words)
+        load_h(1, 0, NODE_BLOCKS)
         nc.sync.dma_start(out=a_sb[:], in_=A_stat.rearrange("(j p) m -> p j m", p=P))
 
         w_words = keep.tile([P, 2, D], U32, align_bytes=64)
@@ -97,8 +95,8 @@ def tile_dynamicgraphattention_kernel(
         h_codes = keep.tile([P, B, N], U32, align_bytes=64)
         h_plane = keep.tile([P, B, N], U8, align_bytes=64)
 
-        def flip_h(b, half):
-            flipped = psum_flip.tile([P, 2, 2 * P], F32)
+        def flip_h(b, half, copy):
+            flipped = psum.tile([P, 2, 2 * P], F32, name="bank")
             for jj in range(2):
                 words = h_sb[:, b, 2 * half + jj, :].bitcast(F32)
                 for u in range(2):
@@ -106,11 +104,10 @@ def tile_dynamicgraphattention_kernel(
                         flipped[:, u, jj * P : (jj + 1) * P], words[:, u : C // 2 : 2], identity[:]
                     )
             nodes = slice(2 * P * half, 2 * P * (half + 1))
-            copy = nc.vector.tensor_copy if half == 0 else nc.scalar.copy
             copy(out=h_pairs[:, b, nodes, :], in_=flipped[:].rearrange("p u n -> p n u"))
 
-        def quantise_h(b, half):
-            nodes = slice(2 * P * half, 2 * P * (half + 1))
+        def quantise_h(b, half0, half1):
+            nodes = slice(2 * P * half0, 2 * P * half1)
             nc.vector.quantize_mx(
                 out=h_codes[:, b, nodes].bitcast(FP8X4),
                 scales=h_plane[:, b, nodes],
@@ -121,10 +118,9 @@ def tile_dynamicgraphattention_kernel(
         qk_codes = keep.tile([P, B, 2, N], U32, align_bytes=64)
         qk_planes = keep.tile([P, B, 2, N], U8, align_bytes=64)
 
-        def project(b, bank, copy):
-            side, j = divmod(bank, NODE_BLOCKS)
+        def project(b, side, j, copy):
             nodes = slice(j * P, (j + 1) * P)
-            acc = psum_proj.tile([P, PACK, P], F32)
+            acc = psum.tile([P, PACK, P], F32, name="bank")
             for t in range(PACK):
                 features = slice(t * P, (t + 1) * P)
                 nc.tensor.matmul_mx(
@@ -138,13 +134,8 @@ def tile_dynamicgraphattention_kernel(
                 )
             copy(out=qk_grouped[:, b, side, nodes, :], in_=acc[:].rearrange("p t n -> p n t"))
 
-        def project_pair_on_scalar(b, pair):
-            project(b, 2 * pair, nc.scalar.copy)
-            project(b, 2 * pair + 1, nc.scalar.copy)
-
-        def quantise_pair(b, pair):
-            side, half = divmod(pair, 2)
-            nodes = slice(2 * P * half, 2 * P * (half + 1))
+        def quantise_qk(b, side, half0, half1):
+            nodes = slice(2 * P * half0, 2 * P * half1)
             nc.vector.quantize_mx(
                 out=qk_codes[:, b, side, nodes].bitcast(FP8X4),
                 scales=qk_planes[:, b, side, nodes],
@@ -158,7 +149,7 @@ def tile_dynamicgraphattention_kernel(
                 out=bias[:], in0=m_sb[:], scalar1=0.0, scalar2=EXCLUDED, op0=ALU.is_le, op1=ALU.mult
             )
 
-        def add_a_stat():
+        def exclude_diagonal():
             for j in range(NODE_BLOCKS):
                 diagonal = a_sb[:, j, j * P : (j + 1) * P]
                 nc.gpsimd.affine_select(
@@ -170,13 +161,21 @@ def tile_dynamicgraphattention_kernel(
                     pattern=[[-1, P]],
                     channel_multiplier=1,
                 )
-            nc.vector.tensor_tensor(out=bias[:], in0=bias[:], in1=a_sb[:], op=ALU.add)
 
-        logits, neg_max, weights, row_sum = {}, {}, {}, {}
+        def add_a_stat(j0, j1):
+            nc.vector.tensor_tensor(
+                out=bias[:, j0:j1], in0=bias[:, j0:j1], in1=a_sb[:, j0:j1], op=ALU.add
+            )
 
-        def logits_and_max(i, b, j):
+        logits, weights = {}, {}
+        neg_max = keep.tile([P, ROW_BLOCKS], F32)
+        row_sum = keep.tile([P, ROW_BLOCKS], F32)
+        inv_sum = keep.tile([P, ROW_BLOCKS], F32)
+
+        def scores_and_logits(i):
+            b, j = divmod(i, NODE_BLOCKS)
             nodes = slice(j * P, (j + 1) * P)
-            score = psum_score.tile([P, N], F32)
+            score = psum.tile([P, N], F32, name="bank")
             for first, (still, moving) in enumerate(((Q_SIDE, K_SIDE), (K_SIDE, Q_SIDE))):
                 nc.tensor.matmul_mx(
                     out=score[:],
@@ -191,58 +190,114 @@ def tile_dynamicgraphattention_kernel(
             nc.vector.scalar_tensor_tensor(
                 out=logits[i][:], in0=score[:], scalar=HALF_SCALE, in1=bias[:, j, :], op0=ALU.mult, op1=ALU.add
             )
-            neg_max[i] = stats.tile([P, 1], F32, name="neg_max")
-            nc.vector.tensor_reduce(out=neg_max[i][:], in_=logits[i][:], axis=AXIS.X, op=ALU.max, negate=True)
+
+        def maximum(i):
+            nc.vector.tensor_reduce(
+                out=neg_max[:, i : i + 1], in_=logits[i][:], axis=AXIS.X, op=ALU.max, negate=True
+            )
 
         def exponentials(i):
             weights[i] = rows.tile([P, N], F32, name="weights")
-            row_sum[i] = stats.tile([P, 1], F32, name="row_sum")
             nc.scalar.activation(
                 out=weights[i][:],
                 in_=logits[i][:],
                 func=ACT.Exp,
-                bias=neg_max[i][:],
+                bias=neg_max[:, i : i + 1],
                 scale=1.0,
-                accum_out=row_sum[i][:],
+                accum_out=row_sum[:, i : i + 1],
             )
 
-        def normalise_and_store(i):
+        def invert_sums(i0, i1):
+            nc.vector.reciprocal(out=inv_sum[:, i0:i1], in_=row_sum[:, i0:i1])
+
+        def normalise_and_store(i, engine):
             b, j = divmod(i, NODE_BLOCKS)
-            inv_sum = stats.tile([P, 1], F32)
-            nc.vector.reciprocal(out=inv_sum[:], in_=row_sum[i][:])
-            nc.gpsimd.tensor_scalar(
-                out=weights[i][:], in0=weights[i][:], scalar1=inv_sum[:], scalar2=0.0, op0=ALU.mult, op1=ALU.add
-            )
+            if engine is nc.scalar:
+                nc.scalar.activation(
+                    out=weights[i][:], in_=weights[i][:], func=ACT.Copy, scale=inv_sum[:, i : i + 1]
+                )
+            else:
+                engine.tensor_scalar(
+                    out=weights[i][:], in0=weights[i][:], scalar1=inv_sum[:, i : i + 1], scalar2=0.0,
+                    op0=ALU.mult, op1=ALU.add,
+                )
             nc.sync.dma_start(out=out[b, j * P : (j + 1) * P, :], in_=weights[i][:])
 
-        for b in range(B):
-            for half in range(2):
-                flip_h(b, half)
-            for half in range(2):
-                quantise_h(b, half)
-        for side in (Q_SIDE, K_SIDE):
-            permute_columns(side)
-        for pair in range(PAIRS):
-            if pair == PAIRS - 1:
-                penalise_excluded()
-            project(0, 2 * pair, nc.scalar.copy)
-            project(0, 2 * pair + 1, nc.scalar.copy if pair % 2 == 0 else nc.vector.tensor_copy)
-            if pair > 0:
-                quantise_pair(0, pair - 1)
-        quantise_pair(0, PAIRS - 1)
-        add_a_stat()
-        for pair in range(PAIRS_AHEAD):
-            project_pair_on_scalar(1, pair)
-        for i in range(B * NODE_BLOCKS):
-            b, j = divmod(i, NODE_BLOCKS)
-            logits_and_max(i, b, j)
-            if i >= LAG:
-                normalise_and_store(i - LAG)
-            if PAIRS_AHEAD + i < PAIRS:
-                project_pair_on_scalar(1, PAIRS_AHEAD + i)
-            exponentials(i)
-            if i in (1, 2):
-                quantise_pair(1, 2 * i - 2)
-                quantise_pair(1, 2 * i - 1)
-        for i in range(B * NODE_BLOCKS - LAG, B * NODE_BLOCKS):
-            normalise_and_store(i)
+        on_scalar, on_vector = nc.scalar.copy, nc.vector.tensor_copy
+
+
+        flip_h(0, 0, on_scalar)
+        permute_columns(Q_SIDE)
+        quantise_h(0, 0, 1)
+        flip_h(0, 1, on_scalar)
+        project(0, Q_SIDE, 0, on_scalar)
+        penalise_excluded()
+        project(0, Q_SIDE, 1, on_scalar)
+        quantise_h(0, 1, 2)
+        permute_columns(K_SIDE)
+        project(0, Q_SIDE, 2, on_scalar)
+        project(0, Q_SIDE, 3, on_scalar)
+        project(0, K_SIDE, 0, on_vector)
+        project(0, K_SIDE, 1, on_vector)
+        flip_h(1, 0, on_scalar)
+        flip_h(1, 1, on_scalar)
+        project(0, K_SIDE, 2, on_scalar)
+        project(0, K_SIDE, 3, on_scalar)
+        exclude_diagonal()
+        quantise_qk(0, Q_SIDE, 0, 2)
+        add_a_stat(0, 2)
+        quantise_h(1, 0, 2)
+        project(1, Q_SIDE, 0, on_scalar)
+        project(1, Q_SIDE, 1, on_scalar)
+        quantise_qk(0, K_SIDE, 0, 1)
+        quantise_qk(0, K_SIDE, 1, 2)
+        add_a_stat(2, 4)
+        scores_and_logits(0)
+        scores_and_logits(1)
+        maximum(0)
+        project(1, Q_SIDE, 2, on_scalar)
+        project(1, Q_SIDE, 3, on_scalar)
+        scores_and_logits(2)
+        maximum(1)
+        project(1, K_SIDE, 0, on_scalar)
+        project(1, K_SIDE, 1, on_scalar)
+        quantise_qk(1, Q_SIDE, 0, 2)
+        project(1, K_SIDE, 2, on_scalar)
+        exponentials(0)
+        project(1, K_SIDE, 3, on_scalar)
+        maximum(2)
+        quantise_qk(1, K_SIDE, 0, 1)
+        scores_and_logits(3)
+        quantise_qk(1, K_SIDE, 1, 2)
+        exponentials(1)
+
+        maximum(3)
+        invert_sums(0, 1)
+        normalise_and_store(0, nc.gpsimd)
+        exponentials(2)
+        invert_sums(1, 3)
+        scores_and_logits(4)
+        scores_and_logits(5)
+        exponentials(3)
+        normalise_and_store(1, nc.scalar)
+        maximum(4)
+        normalise_and_store(2, nc.scalar)
+        invert_sums(3, 4)
+        normalise_and_store(3, nc.gpsimd)
+        scores_and_logits(6)
+        exponentials(4)
+        maximum(5)
+        exponentials(5)
+        scores_and_logits(7)
+        invert_sums(4, 5)
+        normalise_and_store(4, nc.scalar)
+        maximum(6)
+        invert_sums(5, 6)
+        normalise_and_store(5, nc.gpsimd)
+        exponentials(6)
+        maximum(7)
+        exponentials(7)
+        invert_sums(6, 7)
+        normalise_and_store(6, nc.vector)
+        invert_sums(7, 8)
+        normalise_and_store(7, nc.vector)

@@ -39,8 +39,11 @@ def tile_dynamicgraphattention_kernel(
 
         identity = keep.tile([P, P], F32)
         make_identity(nc, identity[:])
-        planes_in = keep.tile([P, 2, D], U8, align_bytes=64)
-        nc.vector.memset(planes_in[:].rearrange("p w n -> p (w n)").bitcast(I32), 0)
+        planes_in = []
+        for side in (Q_SIDE, K_SIDE):
+            plane = keep.tile([P, D], U8, align_bytes=64, name=f"plane_in_{side}")
+            nc.vector.memset(plane[:].bitcast(I32), 0)
+            planes_in.append(plane)
         warm = keep.tile([P, 1], F32)
         nc.vector.memset(warm[:], 0.0)
         nc.scalar.activation(out=warm[:], in_=warm[:], func=ACT.Exp)
@@ -59,7 +62,7 @@ def tile_dynamicgraphattention_kernel(
             by_r = scales[0].rearrange("(Q r) n -> r Q n", r=4)
             for r in range(4):
                 nc.sync.dma_start(
-                    out=planes_in[r:P:32, side, :].bitcast(I32), in_=by_r[r].bitcast(I32)
+                    out=planes_in[side][r:P:32, :].bitcast(I32), in_=by_r[r].bitcast(I32)
                 )
 
         def load_words(side, words):
@@ -72,9 +75,9 @@ def tile_dynamicgraphattention_kernel(
         load_scales(Q_SIDE, Wq_scales)
         load_words(Q_SIDE, Wq_words)
         load_h(0, 2, 4)
-        nc.sync.dma_start(out=m_sb[:], in_=M_mask.rearrange("(j p) m -> p j m", p=P))
-        load_scales(K_SIDE, Wk_scales)
         load_words(K_SIDE, Wk_words)
+        load_scales(K_SIDE, Wk_scales)
+        nc.sync.dma_start(out=m_sb[:], in_=M_mask.rearrange("(j p) m -> p j m", p=P))
         load_h(1, 0, NODE_BLOCKS)
         nc.sync.dma_start(out=a_sb[:], in_=A_stat.rearrange("(j p) m -> p j m", p=P))
 
@@ -88,7 +91,7 @@ def tile_dynamicgraphattention_kernel(
             )
             nc.vector.tensor_copy(
                 out=w_planes[:, side, :].bitcast(I32).rearrange("p (t q r) -> p t q r", t=PACK, r=2),
-                in_=planes_in[:, side, :].bitcast(I32).rearrange("p (q t r) -> p t q r", t=PACK, r=2),
+                in_=planes_in[side][:].bitcast(I32).rearrange("p (q t r) -> p t q r", t=PACK, r=2),
             )
 
         h_pairs = keep.tile([P, B, N, 2], F32, align_bytes=64)
@@ -230,65 +233,67 @@ def tile_dynamicgraphattention_kernel(
         permute_columns(Q_SIDE)
         quantise_h(0, 0, 1)
         flip_h(0, 1, on_scalar)
-        project(0, Q_SIDE, 0, on_scalar)
-        penalise_excluded()
-        project(0, Q_SIDE, 1, on_scalar)
-        quantise_h(0, 1, 2)
         permute_columns(K_SIDE)
+        project(0, Q_SIDE, 0, on_scalar)
+        quantise_h(0, 1, 2)
+        project(0, Q_SIDE, 1, on_vector)
         project(0, Q_SIDE, 2, on_scalar)
+        penalise_excluded()
         project(0, Q_SIDE, 3, on_scalar)
         project(0, K_SIDE, 0, on_vector)
-        project(0, K_SIDE, 1, on_vector)
+        project(0, K_SIDE, 1, on_scalar)
+
         flip_h(1, 0, on_scalar)
-        flip_h(1, 1, on_scalar)
+        quantise_qk(0, Q_SIDE, 0, 2)
+        quantise_qk(0, K_SIDE, 0, 1)
         project(0, K_SIDE, 2, on_scalar)
         project(0, K_SIDE, 3, on_scalar)
         exclude_diagonal()
-        quantise_qk(0, Q_SIDE, 0, 2)
+        quantise_h(1, 0, 1)
+        flip_h(1, 1, on_scalar)
         add_a_stat(0, 2)
-        quantise_h(1, 0, 2)
         project(1, Q_SIDE, 0, on_scalar)
-        project(1, Q_SIDE, 1, on_scalar)
-        quantise_qk(0, K_SIDE, 0, 1)
         quantise_qk(0, K_SIDE, 1, 2)
+        project(1, Q_SIDE, 1, on_scalar)
         add_a_stat(2, 4)
+        quantise_h(1, 1, 2)
+
         scores_and_logits(0)
-        scores_and_logits(1)
-        maximum(0)
         project(1, Q_SIDE, 2, on_scalar)
         project(1, Q_SIDE, 3, on_scalar)
+        maximum(0)
+        scores_and_logits(1)
+        project(1, K_SIDE, 0, on_scalar)
         scores_and_logits(2)
         maximum(1)
-        project(1, K_SIDE, 0, on_scalar)
         project(1, K_SIDE, 1, on_scalar)
         quantise_qk(1, Q_SIDE, 0, 2)
         project(1, K_SIDE, 2, on_scalar)
-        exponentials(0)
         project(1, K_SIDE, 3, on_scalar)
         maximum(2)
-        quantise_qk(1, K_SIDE, 0, 1)
+        exponentials(0)
+        quantise_qk(1, K_SIDE, 0, 2)
         scores_and_logits(3)
-        quantise_qk(1, K_SIDE, 1, 2)
         exponentials(1)
-
-        maximum(3)
+        exponentials(2)
         invert_sums(0, 1)
         normalise_and_store(0, nc.gpsimd)
-        exponentials(2)
-        invert_sums(1, 3)
+        maximum(3)
         scores_and_logits(4)
-        scores_and_logits(5)
+        invert_sums(1, 2)
         exponentials(3)
+        scores_and_logits(5)
         normalise_and_store(1, nc.scalar)
+        invert_sums(2, 3)
         maximum(4)
-        normalise_and_store(2, nc.scalar)
-        invert_sums(3, 4)
-        normalise_and_store(3, nc.gpsimd)
+        normalise_and_store(2, nc.gpsimd)
         scores_and_logits(6)
+        invert_sums(3, 4)
         exponentials(4)
         maximum(5)
-        exponentials(5)
+        normalise_and_store(3, nc.scalar)
         scores_and_logits(7)
+        exponentials(5)
         invert_sums(4, 5)
         normalise_and_store(4, nc.scalar)
         maximum(6)

@@ -154,7 +154,7 @@ def tile_dynamicgraphattention_kernel(
 
         def exclude_diagonal():
             for j in range(NODE_BLOCKS):
-                diagonal = a_sb[:, j, j * P : (j + 1) * P]
+                diagonal = bias[:, j, j * P : (j + 1) * P]
                 nc.gpsimd.affine_select(
                     out=diagonal,
                     in_=diagonal,
@@ -239,28 +239,27 @@ def tile_dynamicgraphattention_kernel(
         project(0, Q_SIDE, 1, on_vector)
         project(0, Q_SIDE, 2, on_scalar)
         penalise_excluded()
+        exclude_diagonal()
         project(0, Q_SIDE, 3, on_scalar)
         project(0, K_SIDE, 0, on_vector)
         project(0, K_SIDE, 1, on_scalar)
-
         flip_h(1, 0, on_scalar)
         quantise_qk(0, Q_SIDE, 0, 2)
         quantise_qk(0, K_SIDE, 0, 1)
         project(0, K_SIDE, 2, on_scalar)
         project(0, K_SIDE, 3, on_scalar)
-        exclude_diagonal()
         quantise_h(1, 0, 1)
         flip_h(1, 1, on_scalar)
-        add_a_stat(0, 2)
         project(1, Q_SIDE, 0, on_scalar)
         quantise_qk(0, K_SIDE, 1, 2)
         project(1, Q_SIDE, 1, on_scalar)
-        add_a_stat(2, 4)
+        add_a_stat(0, 2)
         quantise_h(1, 1, 2)
 
         scores_and_logits(0)
         project(1, Q_SIDE, 2, on_scalar)
         project(1, Q_SIDE, 3, on_scalar)
+        add_a_stat(2, 4)
         maximum(0)
         scores_and_logits(1)
         project(1, K_SIDE, 0, on_scalar)

@@ -22,6 +22,7 @@ TAU = 1.5
 HALF_SCALE = 0.5 / (math.sqrt(C) * TAU)
 EXCLUDED = -1.0e30
 Q_SIDE, K_SIDE = 0, 1
+WARM_UPS = 4
 ROW_BLOCKS = B * NODE_BLOCKS
 
 FLOPS = 2 * B * N * C * (2 * D) + 2 * B * N * N * D
@@ -37,6 +38,11 @@ def tile_dynamicgraphattention_kernel(
         psum = ctx.enter_context(tc.psum_pool(name="psum", bufs=8))
         ctx.enter_context(tc.manual_schedule())
 
+        zeros = keep.tile([P, N], BF16, align_bytes=64)
+        nc.gpsimd.memset(zeros[:].bitcast(U32), 0)
+        spare = psum.tile([P, N], F32, name="bank")
+        for turn in range(WARM_UPS):
+            nc.tensor.matmul(spare[:], lhsT=zeros[:, :P], rhs=zeros[:], start=True, stop=True)
         identity = keep.tile([P, P], F32)
         make_identity(nc, identity[:])
         planes_in = []

@@ -77,14 +77,15 @@ def tile_dynamicgraphattention_kernel(
                 in_=words[0].rearrange("p n t -> p (n t)").bitcast(I32),
             )
 
-        load_h(0, 0, 2)
-        load_scales(Q_SIDE, Wq_scales)
+        load_h(0, 0, 1)
         load_words(Q_SIDE, Wq_words)
+        load_h(0, 1, 2)
+        load_scales(Q_SIDE, Wq_scales)
         load_h(0, 2, 4)
         load_words(K_SIDE, Wk_words)
         load_scales(K_SIDE, Wk_scales)
-        nc.sync.dma_start(out=m_sb[:], in_=M_mask.rearrange("(j p) m -> p j m", p=P))
         load_h(1, 0, NODE_BLOCKS)
+        nc.sync.dma_start(out=m_sb[:], in_=M_mask.rearrange("(j p) m -> p j m", p=P))
         nc.sync.dma_start(out=a_sb[:], in_=A_stat.rearrange("(j p) m -> p j m", p=P))
 
         w_words = keep.tile([P, 2, D], U32, align_bytes=64)
@@ -104,19 +105,21 @@ def tile_dynamicgraphattention_kernel(
         h_codes = keep.tile([P, B, N], U32, align_bytes=64)
         h_plane = keep.tile([P, B, N], U8, align_bytes=64)
 
-        def flip_h(b, half, copy):
+        def flip_h(b, j0, j1, copy):
             flipped = psum.tile([P, 2, 2 * P], F32, name="bank")
-            for jj in range(2):
-                words = h_sb[:, b, 2 * half + jj, :].bitcast(F32)
+            for j in range(j0, j1):
+                words = h_sb[:, b, j, :].bitcast(F32)
                 for u in range(2):
                     nc.tensor.transpose(
-                        flipped[:, u, jj * P : (jj + 1) * P], words[:, u : C // 2 : 2], identity[:]
+                        flipped[:, u, (j - j0) * P : (j - j0 + 1) * P], words[:, u : C // 2 : 2], identity[:]
                     )
-            nodes = slice(2 * P * half, 2 * P * (half + 1))
-            copy(out=h_pairs[:, b, nodes, :], in_=flipped[:].rearrange("p u n -> p n u"))
+            copy(
+                out=h_pairs[:, b, j0 * P : j1 * P, :],
+                in_=flipped[:, :, : (j1 - j0) * P].rearrange("p u n -> p n u"),
+            )
 
-        def quantise_h(b, half0, half1):
-            nodes = slice(2 * P * half0, 2 * P * half1)
+        def quantise_h(b, j0, j1):
+            nodes = slice(j0 * P, j1 * P)
             nc.vector.quantize_mx(
                 out=h_codes[:, b, nodes].bitcast(FP8X4),
                 scales=h_plane[:, b, nodes],
@@ -143,8 +146,8 @@ def tile_dynamicgraphattention_kernel(
                 )
             copy(out=qk_grouped[:, b, side, nodes, :], in_=acc[:].rearrange("p t n -> p n t"))
 
-        def quantise_qk(b, side, half0, half1):
-            nodes = slice(2 * P * half0, 2 * P * half1)
+        def quantise_qk(b, side, j0, j1):
+            nodes = slice(j0 * P, j1 * P)
             nc.vector.quantize_mx(
                 out=qk_codes[:, b, side, nodes].bitcast(FP8X4),
                 scales=qk_planes[:, b, side, nodes],
@@ -235,65 +238,68 @@ def tile_dynamicgraphattention_kernel(
         on_scalar, on_vector = nc.scalar.copy, nc.vector.tensor_copy
 
 
-        flip_h(0, 0, on_scalar)
+        flip_h(0, 0, 1, on_scalar)
         permute_columns(Q_SIDE)
+        flip_h(0, 1, 2, on_scalar)
         quantise_h(0, 0, 1)
-        flip_h(0, 1, on_scalar)
-        permute_columns(K_SIDE)
-        project(0, Q_SIDE, 0, on_scalar)
+        flip_h(0, 2, 3, on_vector)
+        flip_h(0, 3, 4, on_scalar)
         quantise_h(0, 1, 2)
-        project(0, Q_SIDE, 1, on_vector)
-        project(0, Q_SIDE, 2, on_scalar)
-        penalise_excluded()
-        exclude_diagonal()
+        project(0, Q_SIDE, 0, on_scalar)
+        project(0, Q_SIDE, 1, on_scalar)
+        quantise_h(0, 2, 4)
+        permute_columns(K_SIDE)
+        project(0, Q_SIDE, 2, on_vector)
         project(0, Q_SIDE, 3, on_scalar)
         project(0, K_SIDE, 0, on_vector)
         project(0, K_SIDE, 1, on_scalar)
-        flip_h(1, 0, on_scalar)
-        quantise_qk(0, Q_SIDE, 0, 2)
-        quantise_qk(0, K_SIDE, 0, 1)
+        flip_h(1, 0, 2, on_scalar)
+        quantise_qk(0, Q_SIDE, 0, 4)
+        penalise_excluded()
+        exclude_diagonal()
         project(0, K_SIDE, 2, on_scalar)
         project(0, K_SIDE, 3, on_scalar)
-        quantise_h(1, 0, 1)
-        flip_h(1, 1, on_scalar)
+        quantise_h(1, 0, 2)
+        flip_h(1, 2, 4, on_scalar)
+        quantise_qk(0, K_SIDE, 0, 2)
         project(1, Q_SIDE, 0, on_scalar)
-        quantise_qk(0, K_SIDE, 1, 2)
         project(1, Q_SIDE, 1, on_scalar)
+        quantise_qk(0, K_SIDE, 2, 4)
         add_a_stat(0, 2)
-        quantise_h(1, 1, 2)
+        quantise_h(1, 2, 4)
 
         scores_and_logits(0)
         project(1, Q_SIDE, 2, on_scalar)
-        project(1, Q_SIDE, 3, on_scalar)
         add_a_stat(2, 4)
-        maximum(0)
         scores_and_logits(1)
+        project(1, Q_SIDE, 3, on_scalar)
         project(1, K_SIDE, 0, on_scalar)
+        maximum(0)
         scores_and_logits(2)
-        maximum(1)
         project(1, K_SIDE, 1, on_scalar)
-        quantise_qk(1, Q_SIDE, 0, 2)
+        maximum(1)
+        quantise_qk(1, Q_SIDE, 0, 4)
         project(1, K_SIDE, 2, on_scalar)
         project(1, K_SIDE, 3, on_scalar)
-        maximum(2)
-        exponentials(0)
         quantise_qk(1, K_SIDE, 0, 2)
-        scores_and_logits(3)
+        exponentials(0)
+        quantise_qk(1, K_SIDE, 2, 4)
         exponentials(1)
-        exponentials(2)
-        invert_sums(0, 1)
-        normalise_and_store(0, nc.gpsimd)
-        maximum(3)
+        scores_and_logits(3)
+        maximum(2)
         scores_and_logits(4)
-        invert_sums(1, 2)
+        maximum(3)
+        invert_sums(0, 2)
+        normalise_and_store(0, nc.gpsimd)
+        exponentials(2)
         exponentials(3)
         scores_and_logits(5)
         normalise_and_store(1, nc.scalar)
-        invert_sums(2, 3)
+
         maximum(4)
-        normalise_and_store(2, nc.gpsimd)
         scores_and_logits(6)
-        invert_sums(3, 4)
+        invert_sums(2, 4)
+        normalise_and_store(2, nc.gpsimd)
         exponentials(4)
         maximum(5)
         normalise_and_store(3, nc.scalar)

@@ -22,6 +22,7 @@ TAU = 1.5
 HALF_SCALE = 0.5 / (math.sqrt(C) * TAU)
 EXCLUDED = -1.0e30
 Q_SIDE, K_SIDE = 0, 1
+SHARED_ROWS = (5,)
 WARM_UPS = 4
 ROW_BLOCKS = B * NODE_BLOCKS
 
@@ -199,9 +200,16 @@ def tile_dynamicgraphattention_kernel(
                     stop=(first == 1),
                 )
             logits[i] = rows.tile([P, N], F32, name="logits")
-            nc.vector.scalar_tensor_tensor(
-                out=logits[i][:], in0=score[:], scalar=HALF_SCALE, in1=bias[:, j, :], op0=ALU.mult, op1=ALU.add
-            )
+            if i in SHARED_ROWS:
+                nc.scalar.mul(logits[i][:], score[:], HALF_SCALE)
+            else:
+                nc.vector.scalar_tensor_tensor(
+                    out=logits[i][:], in0=score[:], scalar=HALF_SCALE, in1=bias[:, j, :], op0=ALU.mult, op1=ALU.add
+                )
+
+        def add_bias(i):
+            bias_rows = bias[:, i % NODE_BLOCKS, :]
+            nc.gpsimd.tensor_tensor(out=logits[i][:], in0=logits[i][:], in1=bias_rows, op=ALU.add)
 
         def maximum(i):
             nc.vector.tensor_reduce(
@@ -285,35 +293,38 @@ def tile_dynamicgraphattention_kernel(
         exponentials(0)
         quantise_qk(1, K_SIDE, 2, 4)
         exponentials(1)
+
         scores_and_logits(3)
+        invert_sums(0, 1)
+        normalise_and_store(0, nc.scalar)
         maximum(2)
         scores_and_logits(4)
-        maximum(3)
-        invert_sums(0, 2)
-        normalise_and_store(0, nc.gpsimd)
+        invert_sums(1, 2)
+        normalise_and_store(1, nc.gpsimd)
         exponentials(2)
-        exponentials(3)
         scores_and_logits(5)
-        normalise_and_store(1, nc.scalar)
-
-        maximum(4)
+        add_bias(5)
+        maximum(3)
         scores_and_logits(6)
-        invert_sums(2, 4)
-        normalise_and_store(2, nc.gpsimd)
-        exponentials(4)
-        maximum(5)
-        normalise_and_store(3, nc.scalar)
+        invert_sums(2, 3)
+        exponentials(3)
+        normalise_and_store(2, nc.scalar)
+        maximum(4)
+        invert_sums(3, 4)
+        normalise_and_store(3, nc.gpsimd)
         scores_and_logits(7)
-        exponentials(5)
-        invert_sums(4, 5)
-        normalise_and_store(4, nc.scalar)
+        exponentials(4)
         maximum(6)
-        invert_sums(5, 6)
-        normalise_and_store(5, nc.gpsimd)
+        invert_sums(4, 5)
+        normalise_and_store(4, nc.gpsimd)
+        maximum(5)
         exponentials(6)
         maximum(7)
-        exponentials(7)
+        exponentials(5)
         invert_sums(6, 7)
         normalise_and_store(6, nc.vector)
+        exponentials(7)
+        invert_sums(5, 6)
+        normalise_and_store(5, nc.vector)
         invert_sums(7, 8)
         normalise_and_store(7, nc.vector)

@@ -57,7 +57,9 @@ def tile_dynamicgraphattention_kernel(
 
         h_sb = keep.tile([P, B, NODE_BLOCKS, C], BF16)
         words_in = keep.tile([P, 2, D], U32, align_bytes=64)
-        m_sb = keep.tile([P, NODE_BLOCKS, N], BF16)
+        m_flat = keep.tile([P, NODE_BLOCKS * (N + P)], BF16)
+        m_sb = m_flat[:, : NODE_BLOCKS * N].rearrange("p (j m) -> p j m", j=NODE_BLOCKS)
+        m_diagonal = m_flat[:].rearrange("p (j m) -> p j m", j=NODE_BLOCKS)[:, :, :P]
         a_sb = keep.tile([P, NODE_BLOCKS, N], BF16)
 
         def load_h(b, j0, j1):
@@ -86,7 +88,7 @@ def tile_dynamicgraphattention_kernel(
         load_words(K_SIDE, Wk_words)
         load_scales(K_SIDE, Wk_scales)
         load_h(1, 0, NODE_BLOCKS)
-        nc.sync.dma_start(out=m_sb[:], in_=M_mask.rearrange("(j p) m -> p j m", p=P))
+        nc.sync.dma_start(out=m_sb, in_=M_mask.rearrange("(j p) m -> p j m", p=P))
         nc.sync.dma_start(out=a_sb[:], in_=A_stat.rearrange("(j p) m -> p j m", p=P))
 
         w_words = keep.tile([P, 2, D], U32, align_bytes=64)
@@ -159,21 +161,24 @@ def tile_dynamicgraphattention_kernel(
 
         def penalise_excluded():
             nc.vector.tensor_scalar(
-                out=bias[:], in0=m_sb[:], scalar1=0.0, scalar2=EXCLUDED, op0=ALU.is_le, op1=ALU.mult
+                out=bias[:], in0=m_sb, scalar1=0.0, scalar2=EXCLUDED, op0=ALU.is_le, op1=ALU.mult
+            )
+
+        off_diagonal = keep.tile([P, NODE_BLOCKS, P], BF16)
+        nc.gpsimd.memset(off_diagonal[:], 1.0)
+        for j in range(NODE_BLOCKS):
+            nc.gpsimd.affine_select(
+                out=off_diagonal[:, j, :],
+                in_=off_diagonal[:, j, :],
+                compare_op=ALU.not_equal,
+                fill=0.0,
+                base=0,
+                pattern=[[-1, P]],
+                channel_multiplier=1,
             )
 
         def exclude_diagonal():
-            for j in range(NODE_BLOCKS):
-                diagonal = bias[:, j, j * P : (j + 1) * P]
-                nc.gpsimd.affine_select(
-                    out=diagonal,
-                    in_=diagonal,
-                    compare_op=ALU.not_equal,
-                    fill=EXCLUDED,
-                    base=0,
-                    pattern=[[-1, P]],
-                    channel_multiplier=1,
-                )
+            nc.vector.tensor_tensor(out=m_diagonal, in0=m_diagonal, in1=off_diagonal[:], op=ALU.min)
 
         def add_a_stat(j0, j1):
             nc.vector.tensor_tensor(
@@ -263,11 +268,11 @@ def tile_dynamicgraphattention_kernel(
         project(0, K_SIDE, 1, on_scalar)
         flip_h(1, 0, 2, on_scalar)
         quantise_qk(0, Q_SIDE, 0, 4)
-        penalise_excluded()
         exclude_diagonal()
         project(0, K_SIDE, 2, on_scalar)
         project(0, K_SIDE, 3, on_scalar)
         quantise_h(1, 0, 2)
+        penalise_excluded()
         flip_h(1, 2, 4, on_scalar)
         quantise_qk(0, K_SIDE, 0, 2)
         project(1, Q_SIDE, 0, on_scalar)

@@ -22,7 +22,7 @@ TAU = 1.5
 HALF_SCALE = 0.5 / (math.sqrt(C) * TAU)
 EXCLUDED = -1.0e30
 Q_SIDE, K_SIDE = 0, 1
-SHARED_ROWS = (5,)
+SHARED_ROWS = (2, 5)
 WARM_UPS = 4
 ROW_BLOCKS = B * NODE_BLOCKS
 
@@ -41,9 +41,13 @@ def tile_dynamicgraphattention_kernel(
 
         zeros = keep.tile([P, N], BF16, align_bytes=64)
         nc.gpsimd.memset(zeros[:].bitcast(U32), 0)
-        spare = psum.tile([P, N], F32, name="bank")
-        for turn in range(WARM_UPS):
-            nc.tensor.matmul(spare[:], lhsT=zeros[:, :P], rhs=zeros[:], start=True, stop=True)
+
+        def warm_up(turns):
+            spare = psum.tile([P, N], F32, name="bank")
+            for turn in range(turns):
+                nc.tensor.matmul(spare[:], lhsT=zeros[:, :P], rhs=zeros[:], start=True, stop=True)
+
+        warm_up(WARM_UPS)
         identity = keep.tile([P, P], F32)
         make_identity(nc, identity[:])
         planes_in = []
@@ -253,7 +257,9 @@ def tile_dynamicgraphattention_kernel(
 
         flip_h(0, 0, 1, on_scalar)
         permute_columns(Q_SIDE)
+        warm_up(1)
         flip_h(0, 1, 2, on_scalar)
+        warm_up(1)
         quantise_h(0, 0, 1)
         flip_h(0, 2, 3, on_vector)
         flip_h(0, 3, 4, on_scalar)
@@ -278,47 +284,48 @@ def tile_dynamicgraphattention_kernel(
         project(1, Q_SIDE, 0, on_scalar)
         project(1, Q_SIDE, 1, on_scalar)
         quantise_qk(0, K_SIDE, 2, 4)
-        add_a_stat(0, 2)
+        add_a_stat(0, 1)
         quantise_h(1, 2, 4)
+        add_a_stat(1, 2)
 
         scores_and_logits(0)
         project(1, Q_SIDE, 2, on_scalar)
+        project(1, Q_SIDE, 3, on_scalar)
         add_a_stat(2, 4)
         scores_and_logits(1)
-        project(1, Q_SIDE, 3, on_scalar)
         project(1, K_SIDE, 0, on_scalar)
+        project(1, K_SIDE, 1, on_scalar)
         maximum(0)
         scores_and_logits(2)
-        project(1, K_SIDE, 1, on_scalar)
+        add_bias(2)
         maximum(1)
-        quantise_qk(1, Q_SIDE, 0, 4)
         project(1, K_SIDE, 2, on_scalar)
         project(1, K_SIDE, 3, on_scalar)
+        quantise_qk(1, Q_SIDE, 0, 4)
         quantise_qk(1, K_SIDE, 0, 2)
-        exponentials(0)
-        quantise_qk(1, K_SIDE, 2, 4)
-        exponentials(1)
-
         scores_and_logits(3)
-        invert_sums(0, 1)
-        normalise_and_store(0, nc.scalar)
+        warm_up(3)
+        quantise_qk(1, K_SIDE, 2, 4)
+        exponentials(0)
+        exponentials(1)
         maximum(2)
+        maximum(3)
+        invert_sums(0, 2)
+        normalise_and_store(0, nc.gpsimd)
         scores_and_logits(4)
-        invert_sums(1, 2)
-        normalise_and_store(1, nc.gpsimd)
         exponentials(2)
+        normalise_and_store(1, nc.gpsimd)
         scores_and_logits(5)
         add_bias(5)
-        maximum(3)
-        scores_and_logits(6)
-        invert_sums(2, 3)
-        exponentials(3)
-        normalise_and_store(2, nc.scalar)
         maximum(4)
+        exponentials(3)
+        invert_sums(2, 3)
+        normalise_and_store(2, nc.scalar)
+        scores_and_logits(6)
         invert_sums(3, 4)
         normalise_and_store(3, nc.gpsimd)
-        scores_and_logits(7)
         exponentials(4)
+        scores_and_logits(7)
         maximum(6)
         invert_sums(4, 5)
         normalise_and_store(4, nc.gpsimd)

@@ -22,7 +22,7 @@ TAU = 1.5
 HALF_SCALE = 0.5 / (math.sqrt(C) * TAU)
 EXCLUDED = -1.0e30
 Q_SIDE, K_SIDE = 0, 1
-SHARED_ROWS = (2, 5)
+SHARED_ROWS = (3, 5)
 WARM_UPS = 4
 ROW_BLOCKS = B * NODE_BLOCKS
 
@@ -297,35 +297,36 @@ def tile_dynamicgraphattention_kernel(
         project(1, K_SIDE, 1, on_scalar)
         maximum(0)
         scores_and_logits(2)
-        add_bias(2)
         maximum(1)
         project(1, K_SIDE, 2, on_scalar)
         project(1, K_SIDE, 3, on_scalar)
         quantise_qk(1, Q_SIDE, 0, 4)
         quantise_qk(1, K_SIDE, 0, 2)
         scores_and_logits(3)
+        add_bias(3)
         warm_up(3)
         quantise_qk(1, K_SIDE, 2, 4)
         exponentials(0)
-        exponentials(1)
         maximum(2)
-        maximum(3)
-        invert_sums(0, 2)
+        exponentials(1)
+        invert_sums(0, 1)
         normalise_and_store(0, nc.gpsimd)
         scores_and_logits(4)
         exponentials(2)
+        invert_sums(1, 2)
         normalise_and_store(1, nc.gpsimd)
+        maximum(3)
         scores_and_logits(5)
         add_bias(5)
-        maximum(4)
-        exponentials(3)
-        invert_sums(2, 3)
-        normalise_and_store(2, nc.scalar)
         scores_and_logits(6)
+        invert_sums(2, 3)
+        exponentials(3)
+        maximum(4)
+        normalise_and_store(2, nc.scalar)
+        scores_and_logits(7)
         invert_sums(3, 4)
         normalise_and_store(3, nc.gpsimd)
         exponentials(4)
-        scores_and_logits(7)
         maximum(6)
         invert_sums(4, 5)
         normalise_and_store(4, nc.gpsimd)

@@ -274,13 +274,13 @@ def tile_dynamicgraphattention_kernel(
         project(0, K_SIDE, 1, on_scalar)
         flip_h(1, 0, 2, on_scalar)
         quantise_qk(0, Q_SIDE, 0, 4)
+        quantise_qk(0, K_SIDE, 0, 2)
         exclude_diagonal()
         project(0, K_SIDE, 2, on_scalar)
         project(0, K_SIDE, 3, on_scalar)
         quantise_h(1, 0, 2)
         penalise_excluded()
         flip_h(1, 2, 4, on_scalar)
-        quantise_qk(0, K_SIDE, 0, 2)
         project(1, Q_SIDE, 0, on_scalar)
         project(1, Q_SIDE, 1, on_scalar)
         quantise_qk(0, K_SIDE, 2, 4)
@@ -297,7 +297,6 @@ def tile_dynamicgraphattention_kernel(
         project(1, K_SIDE, 1, on_scalar)
         maximum(0)
         scores_and_logits(2)
-        maximum(1)
         project(1, K_SIDE, 2, on_scalar)
         project(1, K_SIDE, 3, on_scalar)
         quantise_qk(1, Q_SIDE, 0, 4)
@@ -307,10 +306,11 @@ def tile_dynamicgraphattention_kernel(
         warm_up(3)
         quantise_qk(1, K_SIDE, 2, 4)
         exponentials(0)
+        maximum(1)
         maximum(2)
-        exponentials(1)
         invert_sums(0, 1)
         normalise_and_store(0, nc.gpsimd)
+        exponentials(1)
         scores_and_logits(4)
         exponentials(2)
         invert_sums(1, 2)

import math
from contextlib import ExitStack

import concourse.mybir as mybir
from concourse.masks import make_identity

F32 = mybir.dt.float32
BF16 = mybir.dt.bfloat16
I32 = mybir.dt.int32
U32 = mybir.dt.uint32
U8 = mybir.dt.uint8
FP8X4 = mybir.dt.float8_e4m3fn_x4
ALU = mybir.AluOpType
ACT = mybir.ActivationFunctionType
AXIS = mybir.AxisListType

P = 128
PACK = 4
B, N, C, D = 2, 512, 512, 512
NODE_BLOCKS = N // P
TAU = 1.5
HALF_SCALE = 0.5 / (math.sqrt(C) * TAU)
EXCLUDED = -1.0e30
Q_SIDE, K_SIDE = 0, 1
SHARED_ROWS = (3, 5)
WARM_UPS = 4
ROW_BLOCKS = B * NODE_BLOCKS

FLOPS = 2 * B * N * C * (2 * D) + 2 * B * N * N * D


def tile_dynamicgraphattention_kernel(
    tc, H_t, A_stat, M_mask, Wq_words, Wq_scales, Wk_words, Wk_scales, out
):
    nc = tc.nc
    with ExitStack() as ctx:
        keep = ctx.enter_context(tc.tile_pool(name="keep", bufs=1))
        rows = ctx.enter_context(tc.tile_pool(name="rows", bufs=ROW_BLOCKS))
        psum = ctx.enter_context(tc.psum_pool(name="psum", bufs=8))
        ctx.enter_context(tc.manual_schedule())

        zeros = keep.tile([P, N], BF16, align_bytes=64)
        nc.gpsimd.memset(zeros[:].bitcast(U32), 0)

        def warm_up(turns):
            spare = psum.tile([P, N], F32, name="bank")
            for turn in range(turns):
                nc.tensor.matmul(spare[:], lhsT=zeros[:, :P], rhs=zeros[:], start=True, stop=True)

        warm_up(WARM_UPS)
        identity = keep.tile([P, P], F32)
        make_identity(nc, identity[:])
        planes_in = []
        for side in (Q_SIDE, K_SIDE):
            plane = keep.tile([P, D], U8, align_bytes=64, name=f"plane_in_{side}")
            nc.vector.memset(plane[:].bitcast(I32), 0)
            planes_in.append(plane)
        warm = keep.tile([P, 1], F32)
        nc.vector.memset(warm[:], 0.0)
        nc.scalar.activation(out=warm[:], in_=warm[:], func=ACT.Exp)

        h_sb = keep.tile([P, B, NODE_BLOCKS, C], BF16)
        words_in = keep.tile([P, 2, D], U32, align_bytes=64)
        m_flat = keep.tile([P, NODE_BLOCKS * (N + P)], BF16)
        m_sb = m_flat[:, : NODE_BLOCKS * N].rearrange("p (j m) -> p j m", j=NODE_BLOCKS)
        m_diagonal = m_flat[:].rearrange("p (j m) -> p j m", j=NODE_BLOCKS)[:, :, :P]
        a_sb = keep.tile([P, NODE_BLOCKS, N], BF16)

        def load_h(b, j0, j1):
            nc.sync.dma_start(
                out=h_sb[:, b, j0:j1], in_=H_t[b, j0 * P : j1 * P].rearrange("(j p) c -> p j c", p=P)
            )

        def load_scales(side, scales):
            by_r = scales[0].rearrange("(Q r) n -> r Q n", r=4)
            for r in range(4):
                nc.sync.dma_start(
                    out=planes_in[side][r:P:32, :].bitcast(I32), in_=by_r[r].bitcast(I32)
                )

        def load_words(side, words):
            nc.sync.dma_start(
                out=words_in[:, side, :].bitcast(I32),
                in_=words[0].rearrange("p n t -> p (n t)").bitcast(I32),
            )

        load_h(0, 0, 1)
        load_words(Q_SIDE, Wq_words)
        load_h(0, 1, 2)
        load_scales(Q_SIDE, Wq_scales)
        load_h(0, 2, 4)
        load_words(K_SIDE, Wk_words)
        load_scales(K_SIDE, Wk_scales)
        load_h(1, 0, NODE_BLOCKS)
        nc.sync.dma_start(out=m_sb, in_=M_mask.rearrange("(j p) m -> p j m", p=P))
        nc.sync.dma_start(out=a_sb[:], in_=A_stat.rearrange("(j p) m -> p j m", p=P))

        w_words = keep.tile([P, 2, D], U32, align_bytes=64)
        w_planes = keep.tile([P, 2, D], U8, align_bytes=64)

        def permute_columns(side):
            nc.vector.tensor_copy(
                out=w_words[:, side, :].bitcast(I32).rearrange("p (t q r) -> p t q r", t=PACK, r=8),
                in_=words_in[:, side, :].bitcast(I32).rearrange("p (q t r) -> p t q r", t=PACK, r=8),
            )
            nc.vector.tensor_copy(
                out=w_planes[:, side, :].bitcast(I32).rearrange("p (t q r) -> p t q r", t=PACK, r=2),
                in_=planes_in[side][:].bitcast(I32).rearrange("p (q t r) -> p t q r", t=PACK, r=2),
            )

        h_pairs = keep.tile([P, B, N, 2], F32, align_bytes=64)
        h_codes = keep.tile([P, B, N], U32, align_bytes=64)
        h_plane = keep.tile([P, B, N], U8, align_bytes=64)

        def flip_h(b, j0, j1, copy):
            flipped = psum.tile([P, 2, 2 * P], F32, name="bank")
            for j in range(j0, j1):
                words = h_sb[:, b, j, :].bitcast(F32)
                for u in range(2):
                    nc.tensor.transpose(
                        flipped[:, u, (j - j0) * P : (j - j0 + 1) * P], words[:, u : C // 2 : 2], identity[:]
                    )
            copy(
                out=h_pairs[:, b, j0 * P : j1 * P, :],
                in_=flipped[:, :, : (j1 - j0) * P].rearrange("p u n -> p n u"),
            )

        def quantise_h(b, j0, j1):
            nodes = slice(j0 * P, j1 * P)
            nc.vector.quantize_mx(
                out=h_codes[:, b, nodes].bitcast(FP8X4),
                scales=h_plane[:, b, nodes],
                in_=h_pairs[:, b, nodes, :].rearrange("p n u -> p (n u)").bitcast(BF16),
            )

        qk_grouped = keep.tile([P, B, 2, N, PACK], BF16, align_bytes=64)
        qk_codes = keep.tile([P, B, 2, N], U32, align_bytes=64)
        qk_planes = keep.tile([P, B, 2, N], U8, align_bytes=64)

        def project(b, side, j, copy):
            nodes = slice(j * P, (j + 1) * P)
            acc = psum.tile([P, PACK, P], F32, name="bank")
            for t in range(PACK):
                features = slice(t * P, (t + 1) * P)
                nc.tensor.matmul_mx(
                    out=acc[:, t, :],
                    lhsT=w_words[:, side, features].bitcast(FP8X4),
                    lhsT_scale=w_planes[:, side, features],
                    rhs=h_codes[:, b, nodes].bitcast(FP8X4),
                    rhs_scale=h_plane[:, b, nodes],
                    start=True,
                    stop=True,
                )
            copy(out=qk_grouped[:, b, side, nodes, :], in_=acc[:].rearrange("p t n -> p n t"))

        def quantise_qk(b, side, j0, j1):
            nodes = slice(j0 * P, j1 * P)
            nc.vector.quantize_mx(
                out=qk_codes[:, b, side, nodes].bitcast(FP8X4),
                scales=qk_planes[:, b, side, nodes],
                in_=qk_grouped[:, b, side, nodes, :].rearrange("p n t -> p (n t)"),
            )

        bias = keep.tile([P, NODE_BLOCKS, N], BF16)

        def penalise_excluded():
            nc.vector.tensor_scalar(
                out=bias[:], in0=m_sb, scalar1=0.0, scalar2=EXCLUDED, op0=ALU.is_le, op1=ALU.mult
            )

        off_diagonal = keep.tile([P, NODE_BLOCKS, P], BF16)
        nc.gpsimd.memset(off_diagonal[:], 1.0)
        for j in range(NODE_BLOCKS):
            nc.gpsimd.affine_select(
                out=off_diagonal[:, j, :],
                in_=off_diagonal[:, j, :],
                compare_op=ALU.not_equal,
                fill=0.0,
                base=0,
                pattern=[[-1, P]],
                channel_multiplier=1,
            )

        def exclude_diagonal():
            nc.vector.tensor_tensor(out=m_diagonal, in0=m_diagonal, in1=off_diagonal[:], op=ALU.min)

        def add_a_stat(j0, j1):
            nc.vector.tensor_tensor(
                out=bias[:, j0:j1], in0=bias[:, j0:j1], in1=a_sb[:, j0:j1], op=ALU.add
            )

        logits, weights = {}, {}
        neg_max = keep.tile([P, ROW_BLOCKS], F32)
        row_sum = keep.tile([P, ROW_BLOCKS], F32)
        inv_sum = keep.tile([P, ROW_BLOCKS], F32)

        def scores_and_logits(i):
            b, j = divmod(i, NODE_BLOCKS)
            nodes = slice(j * P, (j + 1) * P)
            score = psum.tile([P, N], F32, name="bank")
            for first, (still, moving) in enumerate(((Q_SIDE, K_SIDE), (K_SIDE, Q_SIDE))):
                nc.tensor.matmul_mx(
                    out=score[:],
                    lhsT=qk_codes[:, b, still, nodes].bitcast(FP8X4),
                    lhsT_scale=qk_planes[:, b, still, nodes],
                    rhs=qk_codes[:, b, moving, :].bitcast(FP8X4),
                    rhs_scale=qk_planes[:, b, moving, :],
                    start=(first == 0),
                    stop=(first == 1),
                )
            logits[i] = rows.tile([P, N], F32, name="logits")
            if i in SHARED_ROWS:
                nc.scalar.mul(logits[i][:], score[:], HALF_SCALE)
            else:
                nc.vector.scalar_tensor_tensor(
                    out=logits[i][:], in0=score[:], scalar=HALF_SCALE, in1=bias[:, j, :], op0=ALU.mult, op1=ALU.add
                )

        def add_bias(i):
            bias_rows = bias[:, i % NODE_BLOCKS, :]
            nc.gpsimd.tensor_tensor(out=logits[i][:], in0=logits[i][:], in1=bias_rows, op=ALU.add)

        def maximum(i):
            nc.vector.tensor_reduce(
                out=neg_max[:, i : i + 1], in_=logits[i][:], axis=AXIS.X, op=ALU.max, negate=True
            )

        def exponentials(i):
            weights[i] = rows.tile([P, N], F32, name="weights")
            nc.scalar.activation(
                out=weights[i][:],
                in_=logits[i][:],
                func=ACT.Exp,
                bias=neg_max[:, i : i + 1],
                scale=1.0,
                accum_out=row_sum[:, i : i + 1],
            )

        def invert_sums(i0, i1):
            nc.vector.reciprocal(out=inv_sum[:, i0:i1], in_=row_sum[:, i0:i1])

        def normalise_and_store(i, engine):
            b, j = divmod(i, NODE_BLOCKS)
            if engine is nc.scalar:
                nc.scalar.activation(
                    out=weights[i][:], in_=weights[i][:], func=ACT.Copy, scale=inv_sum[:, i : i + 1]
                )
            else:
                engine.tensor_scalar(
                    out=weights[i][:], in0=weights[i][:], scalar1=inv_sum[:, i : i + 1], scalar2=0.0,
                    op0=ALU.mult, op1=ALU.add,
                )
            nc.sync.dma_start(out=out[b, j * P : (j + 1) * P, :], in_=weights[i][:])

        on_scalar, on_vector = nc.scalar.copy, nc.vector.tensor_copy


        flip_h(0, 0, 1, on_scalar)
        permute_columns(Q_SIDE)
        warm_up(1)
        flip_h(0, 1, 2, on_scalar)
        warm_up(1)
        quantise_h(0, 0, 1)
        flip_h(0, 2, 3, on_vector)
        flip_h(0, 3, 4, on_scalar)
        quantise_h(0, 1, 2)
        project(0, Q_SIDE, 0, on_scalar)
        project(0, Q_SIDE, 1, on_scalar)
        quantise_h(0, 2, 4)
        permute_columns(K_SIDE)
        project(0, Q_SIDE, 2, on_vector)
        project(0, Q_SIDE, 3, on_scalar)
        project(0, K_SIDE, 0, on_vector)
        project(0, K_SIDE, 1, on_scalar)
        flip_h(1, 0, 2, on_scalar)
        quantise_qk(0, Q_SIDE, 0, 4)
        quantise_qk(0, K_SIDE, 0, 2)
        exclude_diagonal()
        project(0, K_SIDE, 2, on_scalar)
        project(0, K_SIDE, 3, on_scalar)
        quantise_h(1, 0, 2)
        penalise_excluded()
        flip_h(1, 2, 4, on_scalar)
        project(1, Q_SIDE, 0, on_scalar)
        project(1, Q_SIDE, 1, on_scalar)
        quantise_qk(0, K_SIDE, 2, 4)
        add_a_stat(0, 1)
        quantise_h(1, 2, 4)
        add_a_stat(1, 2)

        scores_and_logits(0)
        project(1, Q_SIDE, 2, on_scalar)
        project(1, Q_SIDE, 3, on_scalar)
        add_a_stat(2, 4)
        scores_and_logits(1)
        project(1, K_SIDE, 0, on_scalar)
        project(1, K_SIDE, 1, on_scalar)
        maximum(0)
        scores_and_logits(2)
        project(1, K_SIDE, 2, on_scalar)
        project(1, K_SIDE, 3, on_scalar)
        quantise_qk(1, Q_SIDE, 0, 4)
        quantise_qk(1, K_SIDE, 0, 2)
        scores_and_logits(3)
        add_bias(3)
        warm_up(3)
        quantise_qk(1, K_SIDE, 2, 4)
        exponentials(0)
        maximum(1)
        maximum(2)
        invert_sums(0, 1)
        normalise_and_store(0, nc.gpsimd)
        exponentials(1)
        scores_and_logits(4)
        exponentials(2)
        invert_sums(1, 2)
        normalise_and_store(1, nc.gpsimd)
        maximum(3)
        scores_and_logits(5)
        add_bias(5)
        scores_and_logits(6)
        invert_sums(2, 3)
        exponentials(3)
        maximum(4)
        normalise_and_store(2, nc.scalar)
        scores_and_logits(7)
        invert_sums(3, 4)
        normalise_and_store(3, nc.gpsimd)
        exponentials(4)
        maximum(6)
        invert_sums(4, 5)
        normalise_and_store(4, nc.gpsimd)
        maximum(5)
        exponentials(6)
        maximum(7)
        exponentials(5)
        invert_sums(6, 7)
        normalise_and_store(6, nc.vector)
        exponentials(7)
        invert_sums(5, 6)
        normalise_and_store(5, nc.vector)
        invert_sums(7, 8)
        normalise_and_store(7, nc.vector)
